import numpy as np
import ml_dtypes


def mxq(x, axis, fmt="e4m3"):
    dtype, down = {"e4m3": (ml_dtypes.float8_e4m3fn, 7), "e5m2": (ml_dtypes.float8_e5m2, 14)}[fmt]
    v = np.moveaxis(np.asarray(x, np.float32).astype(ml_dtypes.bfloat16).astype(np.float64), axis, -1)
    blocks = v.reshape(v.shape[:-1] + (-1, 32))
    amax = np.abs(blocks).max(-1, keepdims=True)
    byte = np.maximum(np.where(amax > 0, np.frexp(amax)[1] - 1 + 127, 0) - down, 1)
    scale = np.exp2(byte - 127.0)
    codes = (blocks / scale).astype(np.float32).astype(dtype).astype(np.float64)
    return np.moveaxis((codes * scale).reshape(v.shape), -1, axis)


WIDE = False


def mx_kscale(k):
    if not WIDE:
        return np.ones(k)
    levels = np.array([10, -10, 5, -5, 0])
    a = np.random.permutation(np.resize(levels, k // 512 * 4)).reshape(k // 512, 4)
    idx = np.arange(k)
    return np.exp2(a[idx // 512, idx % 128 // 32])


BF16 = ml_dtypes.bfloat16


def bf(x):
    return np.asarray(x, np.float32).astype(BF16)


def f64(x):
    return np.asarray(x).astype(np.float64)


E2M1 = np.array([0.0, 0.5, 1.0, 1.5, 2.0, 3.0, 4.0, 6.0, -0.0, -0.5, -1.0, -1.5, -2.0, -3.0, -4.0, -6.0])


def pack_weight(w, fmt):
    k, n = w.shape
    w = f64(bf(w)).reshape(k // 32, 32, n)
    amax = np.abs(w).max(1)
    if fmt == "e4m3":
        byte = np.frexp(amax)[1] - 1 + 127 - 7
    else:
        mant, ex = np.frexp(amax / 6.0)
        byte = np.where(mant > 0.5, ex, ex - 1) + 127
    byte = np.clip(np.where(amax > 0, byte, 1), 1, 254)
    scaled = (w * np.exp2(127.0 - byte)[:, None, :]).reshape(k, n).astype(np.float32)
    by_word = np.ascontiguousarray(scaled.reshape(k // 512, 128, 4, n).transpose(0, 1, 3, 2))
    if fmt == "e4m3":
        words = by_word.astype(ml_dtypes.float8_e4m3fn).view(np.uint8)
    else:
        c = by_word.astype(ml_dtypes.float4_e2m1fn).view(np.uint8) & 0xF
        words = c[..., 0::2] | (c[..., 1::2] << 4)
    return np.ascontiguousarray(words), np.ascontiguousarray(byte.astype(np.uint8).reshape(k // 512, 16, n))


def unpack_weight(words, scales, fmt):
    g, p, n, _ = words.shape
    if fmt == "e4m3":
        vals = np.ascontiguousarray(words).view(ml_dtypes.float8_e4m3fn).astype(np.float64)
    else:
        nib = np.empty((g, p, n, 4), np.uint8)
        nib[..., 0::2] = words & 0xF
        nib[..., 1::2] = words >> 4
        vals = E2M1[nib]
    vals = vals * np.repeat(np.exp2(scales.astype(np.float64) - 127.0), 8, axis=1)[..., None]
    return vals.transpose(0, 1, 3, 2).reshape(g * 512, n)


B, CIN, R, COUT, H, W, D, KS = 1, 16384, 1024, 1024, 8, 4, 4, 3
P = H * W * D
PAD = (KS - 1) // 2
FMT = "e4m3"


def slice_in_dim(t, a, b, axis):
    idx = [slice(None)] * t.ndim
    idx[axis] = slice(a, b)
    return t[tuple(idx)]


def axis_contract(t, U, axis):
    L = t.shape[axis] - (KS - 1)
    rshape = (1, U.shape[1], 1, 1, 1)
    acc = slice_in_dim(t, 0, L, axis) * U[0].reshape(rshape)
    for k in range(1, KS):
        acc = acc + slice_in_dim(t, k, k + L, axis) * U[k].reshape(rshape)
    return acc


def setup_inputs():
    s, t = mx_kscale(CIN), mx_kscale(R)
    x = bf(np.random.standard_normal((B, CIN, H, W, D)) * s[None, :, None, None, None])
    U_kh = bf(np.random.standard_normal((KS, R)) / np.sqrt(KS))
    U_kw = bf(np.random.standard_normal((KS, R)) / np.sqrt(KS))
    U_kd = bf(np.random.standard_normal((KS, R)) / np.sqrt(KS))
    in_words, in_scales = pack_weight(np.random.standard_normal((CIN, R)) / np.sqrt(CIN) / s[:, None] * t[None, :], FMT)
    out_words, out_scales = pack_weight(np.random.standard_normal((R, COUT)) / np.sqrt(R) / t[:, None], FMT)
    bias = bf(np.random.standard_normal(COUT) * 0.5)
    return {"x": x,
            "U_kh": U_kh,
            "U_kw": U_kw,
            "U_kd": U_kd,
            "U_c_in_words": in_words,
            "U_c_in_scales": in_scales,
            "U_c_out_words": out_words,
            "U_c_out_scales": out_scales,
            "bias": bias}


def reference(x, U_kh, U_kw, U_kd, U_c_in_words, U_c_in_scales, U_c_out_words, U_c_out_scales, bias):
    xq = mxq(f64(x), 1, "e4m3").reshape(B, CIN, P)
    y = (unpack_weight(U_c_in_words, U_c_in_scales, FMT).T @ xq).reshape(B, R, H, W, D)
    y = np.pad(y, ((0, 0), (0, 0), (PAD, PAD), (PAD, PAD), (PAD, PAD)))
    y = axis_contract(y, f64(U_kh), 2)
    y = axis_contract(y, f64(U_kw), 3)
    y = axis_contract(y, f64(U_kd), 4)
    out = (unpack_weight(U_c_out_words, U_c_out_scales, FMT).T @ mxq(y, 1, "e4m3").reshape(B, R, P)).reshape(B, COUT, H, W, D)
    return out + f64(bias)[None, :, None, None, None]

@@ -1,0 +1,227 @@
+from contextlib import ExitStack
+
+import concourse.mybir as mybir
+from concourse.masks import make_identity
+
+F32 = mybir.dt.float32
+BF16 = mybir.dt.bfloat16
+U8 = mybir.dt.uint8
+U32 = mybir.dt.uint32
+I32 = mybir.dt.int32
+FP8X4 = mybir.dt.float8_e4m3fn_x4
+MULT = mybir.AluOpType.mult
+ADD = mybir.AluOpType.add
+COPY = mybir.ActivationFunctionType.Copy
+IDENTITY = mybir.ActivationFunctionType.Identity
+
+P = 128
+PACK = 4
+K_PASS = P * PACK
+CIN, RANK, COUT = 16384, 1024, 1024
+POS = 8 * 4 * 4
+TAPS = 3
+HALF = K_PASS
+HALVES = RANK // HALF
+PASSES = CIN // K_PASS
+ROUND = 4
+ROUNDS = PASSES // ROUND
+WHOLE_ROUNDS = 4
+OUT_TILES = COUT // P
+QUADRANTS = 4
+AXES = ((POS, 16), (16, 4), (4, 1))
+
+FLOPS = 2 * POS * RANK * (CIN + COUT) + 5 * len(AXES) * POS * RANK
+
+
+def tile_lowrankconv3d_k_kernel(
+    tc, x, U_kh, U_kw, U_kd, U_c_in_words, U_c_in_scales, U_c_out_words, U_c_out_scales, bias, out
+):
+    nc = tc.nc
+    with ExitStack() as ctx:
+        keep = ctx.enter_context(tc.tile_pool(name="keep", bufs=1))
+        x_pool = ctx.enter_context(tc.tile_pool(name="x_pool", bufs=3))
+        whole_pool = ctx.enter_context(tc.tile_pool(name="whole_pool", bufs=3))
+        half_pool = ctx.enter_context(tc.tile_pool(name="half_pool", bufs=6))
+        work = ctx.enter_context(tc.tile_pool(name="work", bufs=2))
+        psum_acc = ctx.enter_context(tc.psum_pool(name="psum_acc", bufs=1))
+        psum_rank = ctx.enter_context(tc.psum_pool(name="psum_rank", bufs=1))
+        psum_out = ctx.enter_context(tc.psum_pool(name="psum_out", bufs=2))
+
+        x_rounds = x.rearrange("b c h w d -> (b c) (h w d)").rearrange(
+            "(r g p t) n -> r p g (t n)", g=ROUND, p=P, t=PACK
+        )
+        in_words = U_c_in_words.rearrange("g p n t -> g p (n t)").bitcast(I32)
+        in_scales = U_c_in_scales.bitcast(I32)
+        out_words = U_c_out_words.rearrange("g p n t -> g p (n t)").bitcast(I32)
+        out_scales = U_c_out_scales.bitcast(I32)
+        out_tiles = out.rearrange("b (m i) h w d -> i (b m) (h w d)", i=P)
+
+        in_planes = keep.tile([P, ROUNDS, RANK], U8, align_bytes=64)
+        nc.vector.memset(in_planes[:].rearrange("p r n -> p (r n)").bitcast(I32), 0)
+        out_planes = keep.tile([P, COUT], U8, align_bytes=64)
+        nc.vector.memset(out_planes[:].bitcast(I32), 0)
+
+        ident = keep.tile([P, P], F32)
+        make_identity(nc, ident[:])
+        rows_bf = keep.tile([P, HALF + P], BF16)
+        nc.vector.memset(rows_bf[:], 0.0)
+        for f, taps in enumerate((U_kh, U_kw, U_kd)):
+            nc.scalar.dma_start(
+                out=rows_bf[f * TAPS * HALVES : (f + 1) * TAPS * HALVES, 0:HALF],
+                in_=taps.rearrange("k (a c) -> (k a) c", a=HALVES),
+            )
+        nc.scalar.dma_start(out=rows_bf[0:OUT_TILES, HALF:], in_=bias.rearrange("(m i) -> m i", i=P))
+        rows_f32 = keep.tile([P, PACK + 1, P], F32)
+        nc.vector.tensor_copy(
+            out=rows_f32[:, 0:PACK, :], in_=rows_bf[:, 0:HALF].rearrange("q (p t) -> q t p", t=PACK)
+        )
+        nc.vector.tensor_copy(out=rows_f32[:, PACK, :], in_=rows_bf[:, HALF:])
+        taps_ps = psum_out.tile([P, PACK, P], F32, tag="out")
+        for t in range(PACK):
+            nc.tensor.transpose(taps_ps[:, t, :], rows_f32[:, t, :], ident[:])
+        bias_ps = psum_out.tile([P, P], F32, tag="out")
+        nc.tensor.transpose(bias_ps[:], rows_f32[:, PACK, :], ident[:])
+        tap_rows = len(AXES) * TAPS * HALVES
+        taps_sb = keep.tile([P, PACK, tap_rows], F32)
+        nc.vector.tensor_copy(out=taps_sb[:], in_=taps_ps[:, :, 0:tap_rows])
+        bias_sb = keep.tile([P, OUT_TILES], F32)
+        nc.vector.tensor_copy(out=bias_sb[:], in_=bias_ps[:, 0:OUT_TILES])
+
+        x_codes = keep.tile([P, PASSES, POS], U32, align_bytes=64)
+        x_planes = keep.tile([P, PASSES, POS], U8, align_bytes=64)
+        acc = [psum_acc.tile([P, HALF], F32, name="acc%d" % a, tag="acc%d" % a) for a in range(HALVES)]
+
+        def load_and_quantise_x(r):
+            x_raw = x_pool.tile([P, ROUND, PACK, POS], BF16)
+            nc.sync.dma_start(out=x_raw[:].rearrange("p g t n -> p g (t n)"), in_=x_rounds[r])
+            x_grouped = x_pool.tile([P, ROUND, POS, PACK], BF16, align_bytes=64)
+            nc.vector.tensor_copy(out=x_grouped[:], in_=x_raw[:].rearrange("p g t n -> p g n t"))
+            passes = slice(r * ROUND, (r + 1) * ROUND)
+            nc.vector.quantize_mx(
+                out=x_codes[:, passes, :].rearrange("p g n -> p (g n)").bitcast(FP8X4),
+                scales=x_planes[:, passes, :].rearrange("p g n -> p (g n)"),
+                in_=x_grouped[:].rearrange("p g n t -> p (g n t)"),
+            )
+
+        def load_in_scales(r):
+            for quadrant in range(QUADRANTS):
+                first = 32 * quadrant
+                nc.sync.dma_start(
+                    out=in_planes[first : first + PACK * ROUND, r, :].bitcast(I32),
+                    in_=in_scales[r * ROUND : (r + 1) * ROUND, PACK * quadrant : PACK * (quadrant + 1), :],
+                )
+
+        def contract_round(r, a, words):
+            for j in range(ROUND):
+                g = r * ROUND + j
+                nc.tensor.matmul_mx(
+                    out=acc[a][:],
+                    lhsT=x_codes[:, g, :].bitcast(FP8X4),
+                    lhsT_scale=x_planes[:, g, :],
+                    rhs=words[:, j, :].bitcast(FP8X4),
+                    rhs_scale=in_planes[PACK * j : P, r, a * HALF : (a + 1) * HALF],
+                    start=(g == 0),
+                    stop=(g == PASSES - 1),
+                )
+
+        def load_half(r, a):
+            w_half = half_pool.tile([P, ROUND, HALF], U32, align_bytes=64)
+            nc.sync.dma_start(
+                out=w_half[:].bitcast(I32),
+                in_=in_words[r * ROUND : (r + 1) * ROUND, :, a * HALF : (a + 1) * HALF].rearrange("g p n -> p g n"),
+            )
+            return w_half
+
+        y3_codes = keep.tile([P, HALVES, POS], U32, align_bytes=64)
+        y3_planes = keep.tile([P, HALVES, POS], U8, align_bytes=64)
+
+        def filter_and_quantise(a):
+            y0 = work.tile([P, PACK, P], F32)
+            nc.scalar.copy(out=y0[:], in_=acc[a][:].rearrange("q (p t) -> q t p", t=PACK))
+            before = []
+            for t in range(PACK):
+                turned = psum_rank.tile([P, POS], F32, name="turned%d" % t, tag="turned%d" % t)
+                nc.tensor.transpose(turned[:], y0[:, t, :], ident[:])
+                before.append(turned[:])
+            for f, (run, step) in enumerate(AXES):
+                after = work.tile([P, PACK, POS], F32, name="after%d" % f, tag="after%d" % f)
+                for t in range(PACK):
+                    tap = [
+                        taps_sb[:, t, (f * TAPS + k) * HALVES + a : (f * TAPS + k) * HALVES + a + 1]
+                        for k in range(TAPS)
+                    ]
+                    src = before[t].rearrange("p (o i) -> p o i", i=run)
+                    dst = after[:, t, :].rearrange("p (o i) -> p o i", i=run)
+                    nc.scalar.activation(out=dst, in_=src, func=COPY, scale=tap[1])
+                    nc.vector.scalar_tensor_tensor(
+                        out=dst[:, :, step:], in0=src[:, :, : run - step], scalar=tap[0],
+                        in1=dst[:, :, step:], op0=MULT, op1=ADD,
+                    )
+                    nc.vector.scalar_tensor_tensor(
+                        out=dst[:, :, : run - step], in0=src[:, :, step:], scalar=tap[2],
+                        in1=dst[:, :, : run - step], op0=MULT, op1=ADD,
+                    )
+                before = [after[:, t, :] for t in range(PACK)]
+            y3_grouped = work.tile([P, POS, PACK], BF16, align_bytes=64)
+            nc.vector.tensor_copy(out=y3_grouped[:], in_=after[:].rearrange("p t n -> p n t"))
+            nc.vector.quantize_mx(
+                out=y3_codes[:, a, :].bitcast(FP8X4),
+                scales=y3_planes[:, a, :],
+                in_=y3_grouped[:].rearrange("p n t -> p (n t)"),
+            )
+
+        for r in range(WHOLE_ROUNDS):
+            load_and_quantise_x(r)
+            w_whole = whole_pool.tile([P, ROUND, RANK], U32, align_bytes=64)
+            nc.sync.dma_start(
+                out=w_whole[:].bitcast(I32),
+                in_=in_words[r * ROUND : (r + 1) * ROUND].rearrange("g p n -> p g n"),
+            )
+            load_in_scales(r)
+            for a in range(HALVES):
+                contract_round(r, a, w_whole[:, :, a * HALF : (a + 1) * HALF])
+        for r in range(WHOLE_ROUNDS, ROUNDS):
+            load_and_quantise_x(r)
+            w_half = load_half(r, 0)
+            load_in_scales(r)
+            contract_round(r, 0, w_half)
+        for quadrant in range(QUADRANTS):
+            first = 32 * quadrant
+            nc.sync.dma_start(
+                out=out_planes[first : first + PACK * HALVES, :].bitcast(I32),
+                in_=out_scales[:, PACK * quadrant : PACK * (quadrant + 1), :],
+            )
+        filter_and_quantise(0)
+        for r in range(WHOLE_ROUNDS, ROUNDS):
+            w_half = load_half(r, 1)
+            contract_round(r, 1, w_half)
+        uo_words = keep.tile([P, HALVES, COUT], U32, align_bytes=64)
+        nc.sync.dma_start(out=uo_words[:].bitcast(I32), in_=out_words.rearrange("g p n -> p g n"))
+        filter_and_quantise(1)
+
+        out_sb = keep.tile([P, OUT_TILES, POS], F32)
+        tiles_per_bank = HALF // POS
+        for bank in range(OUT_TILES // tiles_per_bank):
+            out_ps = psum_out.tile([P, tiles_per_bank, POS], F32, tag="out")
+            for s in range(tiles_per_bank):
+                m = bank * tiles_per_bank + s
+                for a in range(HALVES):
+                    nc.tensor.matmul_mx(
+                        out=out_ps[:, s, :],
+                        lhsT=uo_words[:, a, m * P : (m + 1) * P].bitcast(FP8X4),
+                        lhsT_scale=out_planes[PACK * a : P, m * P : (m + 1) * P],
+                        rhs=y3_codes[:, a, :].bitcast(FP8X4),
+                        rhs_scale=y3_planes[:, a, :],
+                        start=(a == 0),
+                        stop=(a == HALVES - 1),
+                    )
+            for s in range(tiles_per_bank):
+                m = bank * tiles_per_bank + s
+                if bank % 2 == 0:
+                    nc.vector.tensor_scalar_add(out=out_sb[:, m, :], in0=out_ps[:, s, :], scalar1=bias_sb[:, m : m + 1])
+                else:
+                    nc.scalar.activation(
+                        out=out_sb[:, m, :], in_=out_ps[:, s, :], func=IDENTITY, bias=bias_sb[:, m : m + 1]
+                    )
+            tiles = slice(bank * tiles_per_bank, (bank + 1) * tiles_per_bank)
+            nc.sync.dma_start(out=out_tiles[:, tiles, :], in_=out_sb[:, tiles, :])

@@ -26,6 +26,8 @@ PASSES = CIN // K_PASS
 ROUND = 4
 ROUNDS = PASSES // ROUND
 WHOLE_ROUNDS = 4
+LATE_LOAD = 2
+PSUM_BANKS = 8
 OUT_TILES = COUT // P
 QUADRANTS = 4
 AXES = ((POS, 16), (16, 4), (4, 1))
@@ -41,11 +43,9 @@ def tile_lowrankconv3d_k_kernel(
         keep = ctx.enter_context(tc.tile_pool(name="keep", bufs=1))
         x_pool = ctx.enter_context(tc.tile_pool(name="x_pool", bufs=3))
         whole_pool = ctx.enter_context(tc.tile_pool(name="whole_pool", bufs=3))
-        half_pool = ctx.enter_context(tc.tile_pool(name="half_pool", bufs=6))
+        half_pool = ctx.enter_context(tc.tile_pool(name="half_pool", bufs=12))
         work = ctx.enter_context(tc.tile_pool(name="work", bufs=2))
-        psum_acc = ctx.enter_context(tc.psum_pool(name="psum_acc", bufs=1))
-        psum_rank = ctx.enter_context(tc.psum_pool(name="psum_rank", bufs=1))
-        psum_out = ctx.enter_context(tc.psum_pool(name="psum_out", bufs=2))
+        psum = ctx.enter_context(tc.psum_pool(name="psum", bufs=PSUM_BANKS))
 
         x_rounds = x.rearrange("b c h w d -> (b c) (h w d)").rearrange(
             "(r g p t) n -> r p g (t n)", g=ROUND, p=P, t=PACK
@@ -76,10 +76,10 @@ def tile_lowrankconv3d_k_kernel(
             out=rows_f32[:, 0:PACK, :], in_=rows_bf[:, 0:HALF].rearrange("q (p t) -> q t p", t=PACK)
         )
         nc.vector.tensor_copy(out=rows_f32[:, PACK, :], in_=rows_bf[:, HALF:])
-        taps_ps = psum_out.tile([P, PACK, P], F32, tag="out")
+        taps_ps = psum.tile([P, PACK, P], F32, tag="bank")
         for t in range(PACK):
             nc.tensor.transpose(taps_ps[:, t, :], rows_f32[:, t, :], ident[:])
-        bias_ps = psum_out.tile([P, P], F32, tag="out")
+        bias_ps = psum.tile([P, P], F32, tag="bank")
         nc.tensor.transpose(bias_ps[:], rows_f32[:, PACK, :], ident[:])
         tap_rows = len(AXES) * TAPS * HALVES
         taps_sb = keep.tile([P, PACK, tap_rows], F32)
@@ -89,7 +89,7 @@ def tile_lowrankconv3d_k_kernel(
 
         x_codes = keep.tile([P, PASSES, POS], U32, align_bytes=64)
         x_planes = keep.tile([P, PASSES, POS], U8, align_bytes=64)
-        acc = [psum_acc.tile([P, HALF], F32, name="acc%d" % a, tag="acc%d" % a) for a in range(HALVES)]
+        acc = [psum.tile([P, HALF], F32, name="acc%d" % a, tag="bank") for a in range(HALVES)]
 
         def load_and_quantise_x(r):
             x_raw = x_pool.tile([P, ROUND, PACK, POS], BF16)
@@ -111,36 +111,40 @@ def tile_lowrankconv3d_k_kernel(
                     in_=in_scales[r * ROUND : (r + 1) * ROUND, PACK * quadrant : PACK * (quadrant + 1), :],
                 )
 
-        def contract_round(r, a, words):
-            for j in range(ROUND):
-                g = r * ROUND + j
+        def contract(first_pass, a, words):
+            for j in range(words.shape[1]):
+                g = first_pass + j
+                r, plane = divmod(g, ROUND)
                 nc.tensor.matmul_mx(
                     out=acc[a][:],
                     lhsT=x_codes[:, g, :].bitcast(FP8X4),
                     lhsT_scale=x_planes[:, g, :],
                     rhs=words[:, j, :].bitcast(FP8X4),
-                    rhs_scale=in_planes[PACK * j : P, r, a * HALF : (a + 1) * HALF],
+                    rhs_scale=in_planes[PACK * plane : P, r, a * HALF : (a + 1) * HALF],
                     start=(g == 0),
                     stop=(g == PASSES - 1),
                 )
 
-        def load_half(r, a):
-            w_half = half_pool.tile([P, ROUND, HALF], U32, align_bytes=64)
+        def load_and_contract_half(first_pass, a):
+            w_half = half_pool.tile([P, LATE_LOAD, HALF], U32, align_bytes=64)
             nc.sync.dma_start(
                 out=w_half[:].bitcast(I32),
-                in_=in_words[r * ROUND : (r + 1) * ROUND, :, a * HALF : (a + 1) * HALF].rearrange("g p n -> p g n"),
+                in_=in_words[first_pass : first_pass + LATE_LOAD, :, a * HALF : (a + 1) * HALF].rearrange(
+                    "g p n -> p g n"
+                ),
             )
-            return w_half
+            contract(first_pass, a, w_half)
 
         y3_codes = keep.tile([P, HALVES, POS], U32, align_bytes=64)
         y3_planes = keep.tile([P, HALVES, POS], U8, align_bytes=64)
 
         def filter_and_quantise(a):
             y0 = work.tile([P, PACK, P], F32)
-            nc.scalar.copy(out=y0[:], in_=acc[a][:].rearrange("q (p t) -> q t p", t=PACK))
+            for t in range(PACK):
+                nc.vector.tensor_copy(out=y0[:, t, :], in_=acc[a][:].rearrange("q (p t) -> q t p", t=PACK)[:, t, :])
             before = []
             for t in range(PACK):
-                turned = psum_rank.tile([P, POS], F32, name="turned%d" % t, tag="turned%d" % t)
+                turned = psum.tile([P, POS], F32, name="turned%d" % t, tag="bank")
                 nc.tensor.transpose(turned[:], y0[:, t, :], ident[:])
                 before.append(turned[:])
             for f, (run, step) in enumerate(AXES):
@@ -163,7 +167,10 @@ def tile_lowrankconv3d_k_kernel(
                     )
                 before = [after[:, t, :] for t in range(PACK)]
             y3_grouped = work.tile([P, POS, PACK], BF16, align_bytes=64)
-            nc.vector.tensor_copy(out=y3_grouped[:], in_=after[:].rearrange("p t n -> p n t"))
+            nc.vector.tensor_copy(
+                out=y3_grouped[:, : POS // 2, :], in_=after[:, :, : POS // 2].rearrange("p t n -> p n t")
+            )
+            nc.scalar.copy(out=y3_grouped[:, POS // 2 :, :], in_=after[:, :, POS // 2 :].rearrange("p t n -> p n t"))
             nc.vector.quantize_mx(
                 out=y3_codes[:, a, :].bitcast(FP8X4),
                 scales=y3_planes[:, a, :],
@@ -179,12 +186,12 @@ def tile_lowrankconv3d_k_kernel(
             )
             load_in_scales(r)
             for a in range(HALVES):
-                contract_round(r, a, w_whole[:, :, a * HALF : (a + 1) * HALF])
+                contract(r * ROUND, a, w_whole[:, :, a * HALF : (a + 1) * HALF])
         for r in range(WHOLE_ROUNDS, ROUNDS):
             load_and_quantise_x(r)
-            w_half = load_half(r, 0)
             load_in_scales(r)
-            contract_round(r, 0, w_half)
+            for first_pass in range(r * ROUND, (r + 1) * ROUND, LATE_LOAD):
+                load_and_contract_half(first_pass, 0)
         for quadrant in range(QUADRANTS):
             first = 32 * quadrant
             nc.sync.dma_start(
@@ -192,36 +199,29 @@ def tile_lowrankconv3d_k_kernel(
                 in_=out_scales[:, PACK * quadrant : PACK * (quadrant + 1), :],
             )
         filter_and_quantise(0)
-        for r in range(WHOLE_ROUNDS, ROUNDS):
-            w_half = load_half(r, 1)
-            contract_round(r, 1, w_half)
+        for first_pass in range(WHOLE_ROUNDS * ROUND, PASSES, LATE_LOAD):
+            load_and_contract_half(first_pass, 1)
         uo_words = keep.tile([P, HALVES, COUT], U32, align_bytes=64)
         nc.sync.dma_start(out=uo_words[:].bitcast(I32), in_=out_words.rearrange("g p n -> p g n"))
         filter_and_quantise(1)
 
+        out_ps = [psum.tile([P, POS], F32, name="out_ps%d" % m, tag="bank") for m in range(OUT_TILES)]
+        for a in range(HALVES):
+            for m in range(OUT_TILES):
+                nc.tensor.matmul_mx(
+                    out=out_ps[m][:],
+                    lhsT=uo_words[:, a, m * P : (m + 1) * P].bitcast(FP8X4),
+                    lhsT_scale=out_planes[PACK * a : P, m * P : (m + 1) * P],
+                    rhs=y3_codes[:, a, :].bitcast(FP8X4),
+                    rhs_scale=y3_planes[:, a, :],
+                    start=(a == 0),
+                    stop=(a == HALVES - 1),
+                )
         out_sb = keep.tile([P, OUT_TILES, POS], F32)
-        tiles_per_bank = HALF // POS
-        for bank in range(OUT_TILES // tiles_per_bank):
-            out_ps = psum_out.tile([P, tiles_per_bank, POS], F32, tag="out")
-            for s in range(tiles_per_bank):
-                m = bank * tiles_per_bank + s
-                for a in range(HALVES):
-                    nc.tensor.matmul_mx(
-                        out=out_ps[:, s, :],
-                        lhsT=uo_words[:, a, m * P : (m + 1) * P].bitcast(FP8X4),
-                        lhsT_scale=out_planes[PACK * a : P, m * P : (m + 1) * P],
-                        rhs=y3_codes[:, a, :].bitcast(FP8X4),
-                        rhs_scale=y3_planes[:, a, :],
-                        start=(a == 0),
-                        stop=(a == HALVES - 1),
-                    )
-            for s in range(tiles_per_bank):
-                m = bank * tiles_per_bank + s
-                if bank % 2 == 0:
-                    nc.vector.tensor_scalar_add(out=out_sb[:, m, :], in0=out_ps[:, s, :], scalar1=bias_sb[:, m : m + 1])
-                else:
-                    nc.scalar.activation(
-                        out=out_sb[:, m, :], in_=out_ps[:, s, :], func=IDENTITY, bias=bias_sb[:, m : m + 1]
-                    )
-            tiles = slice(bank * tiles_per_bank, (bank + 1) * tiles_per_bank)
+        for m in range(OUT_TILES):
+            if m % 2 == 0:
+                nc.vector.tensor_scalar_add(out=out_sb[:, m, :], in0=out_ps[m][:], scalar1=bias_sb[:, m : m + 1])
+            else:
+                nc.scalar.activation(out=out_sb[:, m, :], in_=out_ps[m][:], func=IDENTITY, bias=bias_sb[:, m : m + 1])
+        for tiles in (slice(0, OUT_TILES // 2), slice(OUT_TILES // 2, OUT_TILES)):
             nc.sync.dma_start(out=out_tiles[:, tiles, :], in_=out_sb[:, tiles, :])

@@ -58,6 +58,12 @@ def tile_lowrankconv3d_k_kernel(
 
         in_planes = keep.tile([P, ROUNDS, RANK], U8, align_bytes=64)
         nc.vector.memset(in_planes[:].rearrange("p r n -> p (r n)").bitcast(I32), 0)
+        stage = keep.tile([P, QUADRANTS, RANK], U8, align_bytes=64)
+        for quadrant in range(QUADRANTS):
+            nc.sync.dma_start(
+                out=stage[:, quadrant, :].bitcast(I32),
+                in_=in_scales[:, PACK * quadrant : PACK * (quadrant + 1), :],
+            )
         out_planes = keep.tile([P, COUT], U8, align_bytes=64)
         nc.vector.memset(out_planes[:].bitcast(I32), 0)
 
@@ -108,7 +114,7 @@ def tile_lowrankconv3d_k_kernel(
                 first = 32 * quadrant
                 nc.sync.dma_start(
                     out=in_planes[first : first + PACK * ROUND, r, :].bitcast(I32),
-                    in_=in_scales[r * ROUND : (r + 1) * ROUND, PACK * quadrant : PACK * (quadrant + 1), :],
+                    in_=stage[PACK * ROUND * r : PACK * ROUND * (r + 1), quadrant, :].bitcast(I32),
                 )
 
         def contract(first_pass, a, words):

@@ -28,6 +28,9 @@ ROUNDS = PASSES // ROUND
 WHOLE_ROUNDS = 4
 LATE_LOAD = 2
 PSUM_BANKS = 8
+HALF_BANKS = 2
+BANK_RANKS = HALF // HALF_BANKS
+BANK_WORDS = BANK_RANKS // PACK
 OUT_TILES = COUT // P
 QUADRANTS = 4
 AXES = ((POS, 16), (16, 4), (4, 1))
@@ -95,7 +98,10 @@ def tile_lowrankconv3d_k_kernel(
 
         x_codes = keep.tile([P, PASSES, POS], U32, align_bytes=64)
         x_planes = keep.tile([P, PASSES, POS], U8, align_bytes=64)
-        acc = [psum.tile([P, HALF], F32, name="acc%d" % a, tag="bank") for a in range(HALVES)]
+        acc = [
+            [psum.tile([P, BANK_RANKS], F32, name="acc%d_%d" % (a, b), tag="bank") for b in range(HALF_BANKS)]
+            for a in range(HALVES)
+        ]
 
         def load_and_quantise_x(r):
             x_raw = x_pool.tile([P, ROUND, PACK, POS], BF16)
@@ -121,33 +127,39 @@ def tile_lowrankconv3d_k_kernel(
             for j in range(words.shape[1]):
                 g = first_pass + j
                 r, plane = divmod(g, ROUND)
-                nc.tensor.matmul_mx(
-                    out=acc[a][:],
-                    lhsT=x_codes[:, g, :].bitcast(FP8X4),
-                    lhsT_scale=x_planes[:, g, :],
-                    rhs=words[:, j, :].bitcast(FP8X4),
-                    rhs_scale=in_planes[PACK * plane : P, r, a * HALF : (a + 1) * HALF],
-                    start=(g == 0),
-                    stop=(g == PASSES - 1),
-                )
+                for b in range(HALF_BANKS):
+                    cols = slice(b * BANK_RANKS, (b + 1) * BANK_RANKS)
+                    nc.tensor.matmul_mx(
+                        out=acc[a][b][:],
+                        lhsT=x_codes[:, g, :].bitcast(FP8X4),
+                        lhsT_scale=x_planes[:, g, :],
+                        rhs=words[:, j, cols].bitcast(FP8X4),
+                        rhs_scale=in_planes[PACK * plane : P, r, a * HALF + cols.start : a * HALF + cols.stop],
+                        start=(g == 0),
+                        stop=(g == PASSES - 1),
+                    )
 
-        def load_and_contract_half(first_pass, a):
+        def load_and_contract_half(first_pass, passes, a):
             w_half = half_pool.tile([P, LATE_LOAD, HALF], U32, align_bytes=64)
             nc.sync.dma_start(
-                out=w_half[:].bitcast(I32),
-                in_=in_words[first_pass : first_pass + LATE_LOAD, :, a * HALF : (a + 1) * HALF].rearrange(
+                out=w_half[:, :passes, :].bitcast(I32),
+                in_=in_words[first_pass : first_pass + passes, :, a * HALF : (a + 1) * HALF].rearrange(
                     "g p n -> p g n"
                 ),
             )
-            contract(first_pass, a, w_half)
+            contract(first_pass, a, w_half[:, :passes, :])
 
         y3_codes = keep.tile([P, HALVES, POS], U32, align_bytes=64)
         y3_planes = keep.tile([P, HALVES, POS], U8, align_bytes=64)
 
         def filter_and_quantise(a):
             y0 = work.tile([P, PACK, P], F32)
-            for t in range(PACK):
-                nc.vector.tensor_copy(out=y0[:, t, :], in_=acc[a][:].rearrange("q (p t) -> q t p", t=PACK)[:, t, :])
+            for two_t in (slice(0, 2), slice(2, PACK)):
+                for copy, b in ((nc.vector.tensor_copy, 0), (nc.scalar.copy, 1)):
+                    copy(
+                        out=y0[:, two_t, b * BANK_WORDS : (b + 1) * BANK_WORDS],
+                        in_=acc[a][b][:].rearrange("q (p t) -> q t p", t=PACK)[:, two_t, :],
+                    )
             before = []
             for t in range(PACK):
                 turned = psum.tile([P, POS], F32, name="turned%d" % t, tag="bank")
@@ -197,18 +209,20 @@ def tile_lowrankconv3d_k_kernel(
             load_and_quantise_x(r)
             load_in_scales(r)
             for first_pass in range(r * ROUND, (r + 1) * ROUND, LATE_LOAD):
-                load_and_contract_half(first_pass, 0)
+                load_and_contract_half(first_pass, LATE_LOAD, 0)
+        filter_and_quantise(0)
+        for first_pass in range(WHOLE_ROUNDS * ROUND, PASSES - LATE_LOAD, LATE_LOAD):
+            load_and_contract_half(first_pass, LATE_LOAD, 1)
+        for first_pass in range(PASSES - LATE_LOAD, PASSES):
+            load_and_contract_half(first_pass, 1, 1)
+        uo_words = keep.tile([P, HALVES, COUT], U32, align_bytes=64)
+        nc.sync.dma_start(out=uo_words[:].bitcast(I32), in_=out_words.rearrange("g p n -> p g n"))
         for quadrant in range(QUADRANTS):
             first = 32 * quadrant
             nc.sync.dma_start(
                 out=out_planes[first : first + PACK * HALVES, :].bitcast(I32),
                 in_=out_scales[:, PACK * quadrant : PACK * (quadrant + 1), :],
             )
-        filter_and_quantise(0)
-        for first_pass in range(WHOLE_ROUNDS * ROUND, PASSES, LATE_LOAD):
-            load_and_contract_half(first_pass, 1)
-        uo_words = keep.tile([P, HALVES, COUT], U32, align_bytes=64)
-        nc.sync.dma_start(out=uo_words[:].bitcast(I32), in_=out_words.rearrange("g p n -> p g n"))
         filter_and_quantise(1)
 
         out_ps = [psum.tile([P, POS], F32, name="out_ps%d" % m, tag="bank") for m in range(OUT_TILES)]

@@ -32,6 +32,7 @@ HALF_BANKS = 2
 BANK_RANKS = HALF // HALF_BANKS
 BANK_WORDS = BANK_RANKS // PACK
 OUT_TILES = COUT // P
+STORE_TILES = 2
 QUADRANTS = 4
 AXES = ((POS, 16), (16, 4), (4, 1))
 
@@ -167,21 +168,25 @@ def tile_lowrankconv3d_k_kernel(
                 before.append(turned[:])
             for f, (run, step) in enumerate(AXES):
                 after = work.tile([P, PACK, POS], F32, name="after%d" % f, tag="after%d" % f)
+                tap, src, dst = [], [], []
                 for t in range(PACK):
-                    tap = [
+                    tap.append([
                         taps_sb[:, t, (f * TAPS + k) * HALVES + a : (f * TAPS + k) * HALVES + a + 1]
                         for k in range(TAPS)
-                    ]
-                    src = before[t].rearrange("p (o i) -> p o i", i=run)
-                    dst = after[:, t, :].rearrange("p (o i) -> p o i", i=run)
-                    nc.scalar.activation(out=dst, in_=src, func=COPY, scale=tap[1])
+                    ])
+                    src.append(before[t].rearrange("p (o i) -> p o i", i=run))
+                    dst.append(after[:, t, :].rearrange("p (o i) -> p o i", i=run))
+                for t in range(PACK):
+                    nc.scalar.activation(out=dst[t], in_=src[t], func=COPY, scale=tap[t][1])
+                for t in range(PACK):
                     nc.vector.scalar_tensor_tensor(
-                        out=dst[:, :, step:], in0=src[:, :, : run - step], scalar=tap[0],
-                        in1=dst[:, :, step:], op0=MULT, op1=ADD,
+                        out=dst[t][:, :, step:], in0=src[t][:, :, : run - step], scalar=tap[t][0],
+                        in1=dst[t][:, :, step:], op0=MULT, op1=ADD,
                     )
+                for t in range(PACK):
                     nc.vector.scalar_tensor_tensor(
-                        out=dst[:, :, : run - step], in0=src[:, :, step:], scalar=tap[2],
-                        in1=dst[:, :, : run - step], op0=MULT, op1=ADD,
+                        out=dst[t][:, :, : run - step], in0=src[t][:, :, step:], scalar=tap[t][2],
+                        in1=dst[t][:, :, : run - step], op0=MULT, op1=ADD,
                     )
                 before = [after[:, t, :] for t in range(PACK)]
             y3_grouped = work.tile([P, POS, PACK], BF16, align_bytes=64)
@@ -223,6 +228,11 @@ def tile_lowrankconv3d_k_kernel(
                 out=out_planes[first : first + PACK * HALVES, :].bitcast(I32),
                 in_=out_scales[:, PACK * quadrant : PACK * (quadrant + 1), :],
             )
+        ctx.enter_context(
+            tc.manual_schedule(
+                engines={mybir.EngineType.DVE, mybir.EngineType.Activation, mybir.EngineType.PE}
+            )
+        )
         filter_and_quantise(1)
 
         out_ps = [psum.tile([P, POS], F32, name="out_ps%d" % m, tag="bank") for m in range(OUT_TILES)]
@@ -243,5 +253,6 @@ def tile_lowrankconv3d_k_kernel(
                 nc.vector.tensor_scalar_add(out=out_sb[:, m, :], in0=out_ps[m][:], scalar1=bias_sb[:, m : m + 1])
             else:
                 nc.scalar.activation(out=out_sb[:, m, :], in_=out_ps[m][:], func=IDENTITY, bias=bias_sb[:, m : m + 1])
-        for tiles in (slice(0, OUT_TILES // 2), slice(OUT_TILES // 2, OUT_TILES)):
+        for first in range(0, OUT_TILES, STORE_TILES):
+            tiles = slice(first, first + STORE_TILES)
             nc.sync.dma_start(out=out_tiles[:, tiles, :], in_=out_sb[:, tiles, :])

@@ -26,6 +26,7 @@ PASSES = CIN // K_PASS
 ROUND = 4
 ROUNDS = PASSES // ROUND
 WHOLE_ROUNDS = 4
+WHOLE_LOAD = 2
 LATE_LOAD = 2
 PSUM_BANKS = 8
 HALF_BANKS = 2
@@ -46,7 +47,7 @@ def tile_lowrankconv3d_k_kernel(
     with ExitStack() as ctx:
         keep = ctx.enter_context(tc.tile_pool(name="keep", bufs=1))
         x_pool = ctx.enter_context(tc.tile_pool(name="x_pool", bufs=3))
-        whole_pool = ctx.enter_context(tc.tile_pool(name="whole_pool", bufs=3))
+        whole_pool = ctx.enter_context(tc.tile_pool(name="whole_pool", bufs=6))
         half_pool = ctx.enter_context(tc.tile_pool(name="half_pool", bufs=12))
         work = ctx.enter_context(tc.tile_pool(name="work", bufs=2))
         psum = ctx.enter_context(tc.psum_pool(name="psum", bufs=PSUM_BANKS))
@@ -62,12 +63,7 @@ def tile_lowrankconv3d_k_kernel(
 
         in_planes = keep.tile([P, ROUNDS, RANK], U8, align_bytes=64)
         nc.vector.memset(in_planes[:].rearrange("p r n -> p (r n)").bitcast(I32), 0)
-        stage = keep.tile([P, QUADRANTS, RANK], U8, align_bytes=64)
-        for quadrant in range(QUADRANTS):
-            nc.sync.dma_start(
-                out=stage[:, quadrant, :].bitcast(I32),
-                in_=in_scales[:, PACK * quadrant : PACK * (quadrant + 1), :],
-            )
+        stage = keep.tile([P, QUADRANTS // 2, 2, RANK], U8, align_bytes=64)
         out_planes = keep.tile([P, COUT], U8, align_bytes=64)
         nc.vector.memset(out_planes[:].bitcast(I32), 0)
 
@@ -76,11 +72,11 @@ def tile_lowrankconv3d_k_kernel(
         rows_bf = keep.tile([P, HALF + P], BF16)
         nc.vector.memset(rows_bf[:], 0.0)
         for f, taps in enumerate((U_kh, U_kw, U_kd)):
-            nc.scalar.dma_start(
+            nc.gpsimd.dma_start(
                 out=rows_bf[f * TAPS * HALVES : (f + 1) * TAPS * HALVES, 0:HALF],
                 in_=taps.rearrange("k (a c) -> (k a) c", a=HALVES),
             )
-        nc.scalar.dma_start(out=rows_bf[0:OUT_TILES, HALF:], in_=bias.rearrange("(m i) -> m i", i=P))
+        nc.gpsimd.dma_start(out=rows_bf[0:OUT_TILES, HALF:], in_=bias.rearrange("(m i) -> m i", i=P))
         rows_f32 = keep.tile([P, PACK + 1, P], F32)
         nc.vector.tensor_copy(
             out=rows_f32[:, 0:PACK, :], in_=rows_bf[:, 0:HALF].rearrange("q (p t) -> q t p", t=PACK)
@@ -116,18 +112,31 @@ def tile_lowrankconv3d_k_kernel(
                 in_=x_grouped[:].rearrange("p g n t -> p (g n t)"),
             )
 
-        def load_in_scales(r):
-            for quadrant in range(QUADRANTS):
-                first = 32 * quadrant
+        def move_scales(i):
+            step, quadrant = divmod(i, QUADRANTS)
+            half = P // 2 * (quadrant % 2)
+            if step < 2:
                 nc.sync.dma_start(
-                    out=in_planes[first : first + PACK * ROUND, r, :].bitcast(I32),
-                    in_=stage[PACK * ROUND * r : PACK * ROUND * (r + 1), quadrant, :].bitcast(I32),
+                    out=stage[half : half + P // 2, quadrant // 2, step, :].bitcast(I32),
+                    in_=in_scales[
+                        step * PASSES // 2 : (step + 1) * PASSES // 2, PACK * quadrant : PACK * (quadrant + 1), :
+                    ],
+                )
+            else:
+                r = step - 2
+                src = half + PACK * ROUND * r
+                nc.sync.dma_start(
+                    out=in_planes[32 * quadrant : 32 * quadrant + PACK * ROUND, 2 * r : 2 * r + 2, :]
+                    .rearrange("p b n -> p (b n)")
+                    .bitcast(I32),
+                    in_=stage[src : src + PACK * ROUND, quadrant // 2].rearrange("p b n -> p (b n)").bitcast(I32),
                 )
 
         def contract(first_pass, a, words):
             for j in range(words.shape[1]):
                 g = first_pass + j
                 r, plane = divmod(g, ROUND)
+                slot = 2 * (r % WHOLE_ROUNDS) + r // WHOLE_ROUNDS
                 for b in range(HALF_BANKS):
                     cols = slice(b * BANK_RANKS, (b + 1) * BANK_RANKS)
                     nc.tensor.matmul_mx(
@@ -135,7 +144,7 @@ def tile_lowrankconv3d_k_kernel(
                         lhsT=x_codes[:, g, :].bitcast(FP8X4),
                         lhsT_scale=x_planes[:, g, :],
                         rhs=words[:, j, cols].bitcast(FP8X4),
-                        rhs_scale=in_planes[PACK * plane : P, r, a * HALF + cols.start : a * HALF + cols.stop],
+                        rhs_scale=in_planes[PACK * plane : P, slot, a * HALF + cols.start : a * HALF + cols.stop],
                         start=(g == 0),
                         stop=(g == PASSES - 1),
                     )
@@ -200,19 +209,31 @@ def tile_lowrankconv3d_k_kernel(
                 in_=y3_grouped[:].rearrange("p n t -> p (n t)"),
             )
 
-        for r in range(WHOLE_ROUNDS):
-            load_and_quantise_x(r)
-            w_whole = whole_pool.tile([P, ROUND, RANK], U32, align_bytes=64)
+        def load_whole(first_pass):
+            w_whole = whole_pool.tile([P, WHOLE_LOAD, RANK], U32, align_bytes=64)
             nc.sync.dma_start(
                 out=w_whole[:].bitcast(I32),
-                in_=in_words[r * ROUND : (r + 1) * ROUND].rearrange("g p n -> p g n"),
+                in_=in_words[first_pass : first_pass + WHOLE_LOAD].rearrange("g p n -> p g n"),
             )
-            load_in_scales(r)
-            for a in range(HALVES):
-                contract(r * ROUND, a, w_whole[:, :, a * HALF : (a + 1) * HALF])
+            waiting.append((first_pass, w_whole))
+
+        waiting = []
+        large = 0
+        for r in range(WHOLE_ROUNDS):
+            for load, arg in [(load_and_quantise_x, r)] + [
+                (load_whole, first_pass) for first_pass in range(r * ROUND, (r + 1) * ROUND, WHOLE_LOAD)
+            ]:
+                load(arg)
+                move_scales(2 * large)
+                move_scales(2 * large + 1)
+                large += 1
+                ready = (2 * large // QUADRANTS - 2) * ROUND
+                for first_pass, words in [item for item in waiting if item[0] < ready]:
+                    for a in range(HALVES):
+                        contract(first_pass, a, words[:, :, a * HALF : (a + 1) * HALF])
+                waiting = [item for item in waiting if item[0] >= ready]
         for r in range(WHOLE_ROUNDS, ROUNDS):
             load_and_quantise_x(r)
-            load_in_scales(r)
             for first_pass in range(r * ROUND, (r + 1) * ROUND, LATE_LOAD):
                 load_and_contract_half(first_pass, LATE_LOAD, 0)
         filter_and_quantise(0)

@@ -28,6 +28,8 @@ ROUNDS = PASSES // ROUND
 WHOLE_ROUNDS = 4
 WHOLE_LOAD = 2
 LATE_LOAD = 2
+ROUND_LARGE = 1 + ROUND // WHOLE_LOAD
+WHOLE_LARGE = ROUND_LARGE * WHOLE_ROUNDS
 PSUM_BANKS = 8
 HALF_BANKS = 2
 BANK_RANKS = HALF // HALF_BANKS
@@ -63,7 +65,7 @@ def tile_lowrankconv3d_k_kernel(
 
         in_planes = keep.tile([P, ROUNDS, RANK], U8, align_bytes=64)
         nc.vector.memset(in_planes[:].rearrange("p r n -> p (r n)").bitcast(I32), 0)
-        stage = keep.tile([P, QUADRANTS // 2, 2, RANK], U8, align_bytes=64)
+        stage = keep.tile([P, QUADRANTS, RANK], U8, align_bytes=64)
         out_planes = keep.tile([P, COUT], U8, align_bytes=64)
         nc.vector.memset(out_planes[:].bitcast(I32), 0)
 
@@ -113,30 +115,30 @@ def tile_lowrankconv3d_k_kernel(
             )
 
         def move_scales(i):
-            step, quadrant = divmod(i, QUADRANTS)
-            half = P // 2 * (quadrant % 2)
-            if step < 2:
-                nc.sync.dma_start(
-                    out=stage[half : half + P // 2, quadrant // 2, step, :].bitcast(I32),
-                    in_=in_scales[
-                        step * PASSES // 2 : (step + 1) * PASSES // 2, PACK * quadrant : PACK * (quadrant + 1), :
-                    ],
-                )
-            else:
-                r = step - 2
-                src = half + PACK * ROUND * r
-                nc.sync.dma_start(
-                    out=in_planes[32 * quadrant : 32 * quadrant + PACK * ROUND, 2 * r : 2 * r + 2, :]
-                    .rearrange("p b n -> p (b n)")
-                    .bitcast(I32),
-                    in_=stage[src : src + PACK * ROUND, quadrant // 2].rearrange("p b n -> p (b n)").bitcast(I32),
-                )
+            step, pair = divmod(i, 2)
+            for quadrant in (pair, pair + 2):
+                if step == 0:
+                    nc.sync.dma_start(
+                        out=stage[:, quadrant, :].bitcast(I32),
+                        in_=in_scales[:, PACK * quadrant : PACK * (quadrant + 1), :],
+                    )
+                else:
+                    r = step - 1
+                    nc.sync.dma_start(
+                        out=in_planes[32 * quadrant : 32 * quadrant + PACK * ROUND, r, :].bitcast(I32),
+                        in_=stage[PACK * ROUND * r : PACK * ROUND * (r + 1), quadrant, :].bitcast(I32),
+                    )
+
+        def after_large(i):
+            if i < WHOLE_LARGE:
+                move_scales(i)
+            elif i % 2 == 0:
+                move_scales(WHOLE_LARGE + (i - WHOLE_LARGE) // 2)
 
         def contract(first_pass, a, words):
             for j in range(words.shape[1]):
                 g = first_pass + j
                 r, plane = divmod(g, ROUND)
-                slot = 2 * (r % WHOLE_ROUNDS) + r // WHOLE_ROUNDS
                 for b in range(HALF_BANKS):
                     cols = slice(b * BANK_RANKS, (b + 1) * BANK_RANKS)
                     nc.tensor.matmul_mx(
@@ -144,12 +146,12 @@ def tile_lowrankconv3d_k_kernel(
                         lhsT=x_codes[:, g, :].bitcast(FP8X4),
                         lhsT_scale=x_planes[:, g, :],
                         rhs=words[:, j, cols].bitcast(FP8X4),
-                        rhs_scale=in_planes[PACK * plane : P, slot, a * HALF + cols.start : a * HALF + cols.stop],
+                        rhs_scale=in_planes[PACK * plane : P, r, a * HALF + cols.start : a * HALF + cols.stop],
                         start=(g == 0),
                         stop=(g == PASSES - 1),
                     )
 
-        def load_and_contract_half(first_pass, passes, a):
+        def load_half(first_pass, passes, a):
             w_half = half_pool.tile([P, LATE_LOAD, HALF], U32, align_bytes=64)
             nc.sync.dma_start(
                 out=w_half[:, :passes, :].bitcast(I32),
@@ -157,7 +159,7 @@ def tile_lowrankconv3d_k_kernel(
                     "g p n -> p g n"
                 ),
             )
-            contract(first_pass, a, w_half[:, :passes, :])
+            return w_half[:, :passes, :]
 
         y3_codes = keep.tile([P, HALVES, POS], U32, align_bytes=64)
         y3_planes = keep.tile([P, HALVES, POS], U8, align_bytes=64)
@@ -218,29 +220,32 @@ def tile_lowrankconv3d_k_kernel(
             waiting.append((first_pass, w_whole))
 
         waiting = []
-        large = 0
         for r in range(WHOLE_ROUNDS):
-            for load, arg in [(load_and_quantise_x, r)] + [
-                (load_whole, first_pass) for first_pass in range(r * ROUND, (r + 1) * ROUND, WHOLE_LOAD)
-            ]:
+            for i, (load, arg) in enumerate(
+                [(load_and_quantise_x, r)]
+                + [(load_whole, first_pass) for first_pass in range(r * ROUND, (r + 1) * ROUND, WHOLE_LOAD)]
+            ):
                 load(arg)
-                move_scales(2 * large)
-                move_scales(2 * large + 1)
-                large += 1
-                ready = (2 * large // QUADRANTS - 2) * ROUND
+                large = ROUND_LARGE * r + i
+                after_large(large)
+                ready = ((large + 1) // 2 - 1) * ROUND
                 for first_pass, words in [item for item in waiting if item[0] < ready]:
                     for a in range(HALVES):
                         contract(first_pass, a, words[:, :, a * HALF : (a + 1) * HALF])
                 waiting = [item for item in waiting if item[0] >= ready]
         for r in range(WHOLE_ROUNDS, ROUNDS):
             load_and_quantise_x(r)
-            for first_pass in range(r * ROUND, (r + 1) * ROUND, LATE_LOAD):
-                load_and_contract_half(first_pass, LATE_LOAD, 0)
+            after_large(ROUND_LARGE * r)
+            for i in range(ROUND // LATE_LOAD):
+                first_pass = r * ROUND + i * LATE_LOAD
+                words = load_half(first_pass, LATE_LOAD, 0)
+                after_large(ROUND_LARGE * r + 1 + i)
+                contract(first_pass, 0, words)
         filter_and_quantise(0)
         for first_pass in range(WHOLE_ROUNDS * ROUND, PASSES - LATE_LOAD, LATE_LOAD):
-            load_and_contract_half(first_pass, LATE_LOAD, 1)
+            contract(first_pass, 1, load_half(first_pass, LATE_LOAD, 1))
         for first_pass in range(PASSES - LATE_LOAD, PASSES):
-            load_and_contract_half(first_pass, 1, 1)
+            contract(first_pass, 1, load_half(first_pass, 1, 1))
         uo_words = keep.tile([P, HALVES, COUT], U32, align_bytes=64)
         nc.sync.dma_start(out=uo_words[:].bitcast(I32), in_=out_words.rearrange("g p n -> p g n"))
         for quadrant in range(QUADRANTS):

@@ -37,7 +37,8 @@ BANK_WORDS = BANK_RANKS // PACK
 OUT_TILES = COUT // P
 STORE_TILES = 2
 QUADRANTS = 4
-AXES = ((POS, 16), (16, 4), (4, 1))
+H, W, D = 8, 4, 4
+AXES = ((1, POS, D * H), (2, D * H, H), (0, H, 1))
 
 FLOPS = 2 * POS * RANK * (CIN + COUT) + 5 * len(AXES) * POS * RANK
 
@@ -71,6 +72,10 @@ def tile_lowrankconv3d_k_kernel(
 
         ident = keep.tile([P, P], F32)
         make_identity(nc, ident[:])
+        reorder = keep.tile([P, P], F32)
+        nc.vector.tensor_copy(
+            out=reorder[:].rearrange("q (o h) -> q o h", h=H), in_=ident[:].rearrange("q (h o) -> q o h", h=H)
+        )
         rows_bf = keep.tile([P, HALF + P], BF16)
         nc.vector.memset(rows_bf[:], 0.0)
         for f, taps in enumerate((U_kh, U_kw, U_kd)):
@@ -175,9 +180,9 @@ def tile_lowrankconv3d_k_kernel(
             before = []
             for t in range(PACK):
                 turned = psum.tile([P, POS], F32, name="turned%d" % t, tag="bank")
-                nc.tensor.transpose(turned[:], y0[:, t, :], ident[:])
+                nc.tensor.transpose(turned[:], y0[:, t, :], reorder[:])
                 before.append(turned[:])
-            for f, (run, step) in enumerate(AXES):
+            for stage_no, (f, run, step) in enumerate(AXES):
                 after = work.tile([P, PACK, POS], F32, name="after%d" % f, tag="after%d" % f)
                 tap, src, dst = [], [], []
                 for t in range(PACK):
@@ -187,19 +192,24 @@ def tile_lowrankconv3d_k_kernel(
                     ])
                     src.append(before[t].rearrange("p (o i) -> p o i", i=run))
                     dst.append(after[:, t, :].rearrange("p (o i) -> p o i", i=run))
-                for t in range(PACK):
-                    nc.scalar.activation(out=dst[t], in_=src[t], func=COPY, scale=tap[t][1])
-                for t in range(PACK):
-                    nc.vector.scalar_tensor_tensor(
-                        out=dst[t][:, :, step:], in0=src[t][:, :, : run - step], scalar=tap[t][0],
-                        in1=dst[t][:, :, step:], op0=MULT, op1=ADD,
-                    )
-                for t in range(PACK):
-                    nc.vector.scalar_tensor_tensor(
-                        out=dst[t][:, :, : run - step], in0=src[t][:, :, step:], scalar=tap[t][2],
-                        in1=dst[t][:, :, : run - step], op0=MULT, op1=ADD,
-                    )
+                for pair in (range(0, 2), range(2, PACK)):
+                    for t in pair:
+                        nc.scalar.activation(out=dst[t], in_=src[t], func=COPY, scale=tap[t][1])
+                    for t in pair:
+                        nc.vector.scalar_tensor_tensor(
+                            out=dst[t][:, :, step:], in0=src[t][:, :, : run - step], scalar=tap[t][0],
+                            in1=dst[t][:, :, step:], op0=MULT, op1=ADD,
+                        )
+                    for t in pair:
+                        nc.vector.scalar_tensor_tensor(
+                            out=dst[t][:, :, : run - step], in0=src[t][:, :, step:], scalar=tap[t][2],
+                            in1=dst[t][:, :, : run - step], op0=MULT, op1=ADD,
+                        )
                 before = [after[:, t, :] for t in range(PACK)]
+                if a == HALVES - 1 and stage_no > 0:
+                    warm = psum.tile([P, POS], F32, tag="bank")
+                    for t in range(PACK if stage_no == 1 else 2):
+                        nc.tensor.matmul(warm[:], lhsT=ident[:], rhs=before[t], start=True, stop=True)
             y3_grouped = work.tile([P, POS, PACK], BF16, align_bytes=64)
             nc.vector.tensor_copy(
                 out=y3_grouped[:, : POS // 2, :], in_=after[:, :, : POS // 2].rearrange("p t n -> p n t")
@@ -275,10 +285,12 @@ def tile_lowrankconv3d_k_kernel(
                 )
         out_sb = keep.tile([P, OUT_TILES, POS], F32)
         for m in range(OUT_TILES):
+            src = out_ps[m][:].rearrange("i (o h) -> i h o", h=H)
+            dst = out_sb[:, m, :].rearrange("i (h o) -> i h o", h=H)
             if m % 2 == 0:
-                nc.vector.tensor_scalar_add(out=out_sb[:, m, :], in0=out_ps[m][:], scalar1=bias_sb[:, m : m + 1])
+                nc.vector.tensor_scalar_add(out=dst, in0=src, scalar1=bias_sb[:, m : m + 1])
             else:
-                nc.scalar.activation(out=out_sb[:, m, :], in_=out_ps[m][:], func=IDENTITY, bias=bias_sb[:, m : m + 1])
+                nc.scalar.activation(out=dst, in_=src, func=IDENTITY, bias=bias_sb[:, m : m + 1])
         for first in range(0, OUT_TILES, STORE_TILES):
             tiles = slice(first, first + STORE_TILES)
             nc.sync.dma_start(out=out_tiles[:, tiles, :], in_=out_sb[:, tiles, :])

@@ -27,7 +27,7 @@ ROUND = 4
 ROUNDS = PASSES // ROUND
 WHOLE_ROUNDS = 4
 WHOLE_LOAD = 2
-LATE_LOAD = 2
+LATE_LOAD = 4
 ROUND_LARGE = 1 + ROUND // WHOLE_LOAD
 WHOLE_LARGE = ROUND_LARGE * WHOLE_ROUNDS
 PSUM_BANKS = 8
@@ -51,7 +51,7 @@ def tile_lowrankconv3d_k_kernel(
         keep = ctx.enter_context(tc.tile_pool(name="keep", bufs=1))
         x_pool = ctx.enter_context(tc.tile_pool(name="x_pool", bufs=3))
         whole_pool = ctx.enter_context(tc.tile_pool(name="whole_pool", bufs=6))
-        half_pool = ctx.enter_context(tc.tile_pool(name="half_pool", bufs=12))
+        half_pool = ctx.enter_context(tc.tile_pool(name="half_pool", bufs=7))
         work = ctx.enter_context(tc.tile_pool(name="work", bufs=2))
         psum = ctx.enter_context(tc.psum_pool(name="psum", bufs=PSUM_BANKS))
 
@@ -135,10 +135,8 @@ def tile_lowrankconv3d_k_kernel(
                     )
 
         def after_large(i):
-            if i < WHOLE_LARGE:
+            if i < 2 * (1 + ROUNDS):
                 move_scales(i)
-            elif i % 2 == 0:
-                move_scales(WHOLE_LARGE + (i - WHOLE_LARGE) // 2)
 
         def contract(first_pass, a, words):
             for j in range(words.shape[1]):
@@ -245,17 +243,17 @@ def tile_lowrankconv3d_k_kernel(
                 waiting = [item for item in waiting if item[0] >= ready]
         for r in range(WHOLE_ROUNDS, ROUNDS):
             load_and_quantise_x(r)
-            after_large(ROUND_LARGE * r)
-            for i in range(ROUND // LATE_LOAD):
-                first_pass = r * ROUND + i * LATE_LOAD
-                words = load_half(first_pass, LATE_LOAD, 0)
-                after_large(ROUND_LARGE * r + 1 + i)
+            after_large(large + 1)
+            large += 2
+            for first_pass, passes in [(r * ROUND, 4)] if r < ROUNDS - 1 else [(PASSES - 4, 2), (PASSES - 2, 2)]:
+                words = load_half(first_pass, passes, 0)
+                after_large(large)
                 contract(first_pass, 0, words)
         filter_and_quantise(0)
-        for first_pass in range(WHOLE_ROUNDS * ROUND, PASSES - LATE_LOAD, LATE_LOAD):
+        for first_pass in range(WHOLE_ROUNDS * ROUND, PASSES - ROUND, LATE_LOAD):
             contract(first_pass, 1, load_half(first_pass, LATE_LOAD, 1))
-        for first_pass in range(PASSES - LATE_LOAD, PASSES):
-            contract(first_pass, 1, load_half(first_pass, 1, 1))
+        for first_pass, passes in ((PASSES - 4, 2), (PASSES - 2, 1), (PASSES - 1, 1)):
+            contract(first_pass, 1, load_half(first_pass, passes, 1))
         uo_words = keep.tile([P, HALVES, COUT], U32, align_bytes=64)
         nc.sync.dma_start(out=uo_words[:].bitcast(I32), in_=out_words.rearrange("g p n -> p g n"))
         for quadrant in range(QUADRANTS):

from contextlib import ExitStack

import concourse.mybir as mybir
from concourse.masks import make_identity

F32 = mybir.dt.float32
BF16 = mybir.dt.bfloat16
U8 = mybir.dt.uint8
U32 = mybir.dt.uint32
I32 = mybir.dt.int32
FP8X4 = mybir.dt.float8_e4m3fn_x4
MULT = mybir.AluOpType.mult
ADD = mybir.AluOpType.add
COPY = mybir.ActivationFunctionType.Copy
IDENTITY = mybir.ActivationFunctionType.Identity

P = 128
PACK = 4
K_PASS = P * PACK
CIN, RANK, COUT = 16384, 1024, 1024
POS = 8 * 4 * 4
TAPS = 3
HALF = K_PASS
HALVES = RANK // HALF
PASSES = CIN // K_PASS
ROUND = 4
ROUNDS = PASSES // ROUND
WHOLE_ROUNDS = 4
WHOLE_LOAD = 2
LATE_LOAD = 4
ROUND_LARGE = 1 + ROUND // WHOLE_LOAD
WHOLE_LARGE = ROUND_LARGE * WHOLE_ROUNDS
PSUM_BANKS = 8
HALF_BANKS = 2
BANK_RANKS = HALF // HALF_BANKS
BANK_WORDS = BANK_RANKS // PACK
OUT_TILES = COUT // P
STORE_TILES = 2
QUADRANTS = 4
H, W, D = 8, 4, 4
AXES = ((1, POS, D * H), (2, D * H, H), (0, H, 1))

FLOPS = 2 * POS * RANK * (CIN + COUT) + 5 * len(AXES) * POS * RANK


def tile_lowrankconv3d_k_kernel(
    tc, x, U_kh, U_kw, U_kd, U_c_in_words, U_c_in_scales, U_c_out_words, U_c_out_scales, bias, out
):
    nc = tc.nc
    with ExitStack() as ctx:
        keep = ctx.enter_context(tc.tile_pool(name="keep", bufs=1))
        x_pool = ctx.enter_context(tc.tile_pool(name="x_pool", bufs=3))
        whole_pool = ctx.enter_context(tc.tile_pool(name="whole_pool", bufs=6))
        half_pool = ctx.enter_context(tc.tile_pool(name="half_pool", bufs=7))
        work = ctx.enter_context(tc.tile_pool(name="work", bufs=2))
        psum = ctx.enter_context(tc.psum_pool(name="psum", bufs=PSUM_BANKS))

        x_rounds = x.rearrange("b c h w d -> (b c) (h w d)").rearrange(
            "(r g p t) n -> r p g (t n)", g=ROUND, p=P, t=PACK
        )
        in_words = U_c_in_words.rearrange("g p n t -> g p (n t)").bitcast(I32)
        in_scales = U_c_in_scales.bitcast(I32)
        out_words = U_c_out_words.rearrange("g p n t -> g p (n t)").bitcast(I32)
        out_scales = U_c_out_scales.bitcast(I32)
        out_tiles = out.rearrange("b (m i) h w d -> i (b m) (h w d)", i=P)

        in_planes = keep.tile([P, ROUNDS, RANK], U8, align_bytes=64)
        nc.vector.memset(in_planes[:].rearrange("p r n -> p (r n)").bitcast(I32), 0)
        stage = keep.tile([P, QUADRANTS, RANK], U8, align_bytes=64)
        out_planes = keep.tile([P, COUT], U8, align_bytes=64)
        nc.vector.memset(out_planes[:].bitcast(I32), 0)

        ident = keep.tile([P, P], F32)
        make_identity(nc, ident[:])
        reorder = keep.tile([P, P], F32)
        nc.vector.tensor_copy(
            out=reorder[:].rearrange("q (o h) -> q o h", h=H), in_=ident[:].rearrange("q (h o) -> q o h", h=H)
        )
        rows_bf = keep.tile([P, HALF + P], BF16)
        nc.vector.memset(rows_bf[:], 0.0)
        for f, taps in enumerate((U_kh, U_kw, U_kd)):
            nc.gpsimd.dma_start(
                out=rows_bf[f * TAPS * HALVES : (f + 1) * TAPS * HALVES, 0:HALF],
                in_=taps.rearrange("k (a c) -> (k a) c", a=HALVES),
            )
        nc.gpsimd.dma_start(out=rows_bf[0:OUT_TILES, HALF:], in_=bias.rearrange("(m i) -> m i", i=P))
        rows_f32 = keep.tile([P, PACK + 1, P], F32)
        nc.vector.tensor_copy(
            out=rows_f32[:, 0:PACK, :], in_=rows_bf[:, 0:HALF].rearrange("q (p t) -> q t p", t=PACK)
        )
        nc.vector.tensor_copy(out=rows_f32[:, PACK, :], in_=rows_bf[:, HALF:])
        taps_ps = psum.tile([P, PACK, P], F32, tag="bank")
        for t in range(PACK):
            nc.tensor.transpose(taps_ps[:, t, :], rows_f32[:, t, :], ident[:])
        bias_ps = psum.tile([P, P], F32, tag="bank")
        nc.tensor.transpose(bias_ps[:], rows_f32[:, PACK, :], ident[:])
        tap_rows = len(AXES) * TAPS * HALVES
        taps_sb = keep.tile([P, PACK, tap_rows], F32)
        nc.vector.tensor_copy(out=taps_sb[:], in_=taps_ps[:, :, 0:tap_rows])
        bias_sb = keep.tile([P, OUT_TILES], F32)
        nc.vector.tensor_copy(out=bias_sb[:], in_=bias_ps[:, 0:OUT_TILES])

        x_codes = keep.tile([P, PASSES, POS], U32, align_bytes=64)
        x_planes = keep.tile([P, PASSES, POS], U8, align_bytes=64)
        acc = [
            [psum.tile([P, BANK_RANKS], F32, name="acc%d_%d" % (a, b), tag="bank") for b in range(HALF_BANKS)]
            for a in range(HALVES)
        ]

        def load_and_quantise_x(r):
            x_raw = x_pool.tile([P, ROUND, PACK, POS], BF16)
            nc.sync.dma_start(out=x_raw[:].rearrange("p g t n -> p g (t n)"), in_=x_rounds[r])
            x_grouped = x_pool.tile([P, ROUND, POS, PACK], BF16, align_bytes=64)
            nc.vector.tensor_copy(out=x_grouped[:], in_=x_raw[:].rearrange("p g t n -> p g n t"))
            passes = slice(r * ROUND, (r + 1) * ROUND)
            nc.vector.quantize_mx(
                out=x_codes[:, passes, :].rearrange("p g n -> p (g n)").bitcast(FP8X4),
                scales=x_planes[:, passes, :].rearrange("p g n -> p (g n)"),
                in_=x_grouped[:].rearrange("p g n t -> p (g n t)"),
            )

        def move_scales(i):
            step, pair = divmod(i, 2)
            for quadrant in (pair, pair + 2):
                if step == 0:
                    nc.sync.dma_start(
                        out=stage[:, quadrant, :].bitcast(I32),
                        in_=in_scales[:, PACK * quadrant : PACK * (quadrant + 1), :],
                    )
                else:
                    r = step - 1
                    nc.sync.dma_start(
                        out=in_planes[32 * quadrant : 32 * quadrant + PACK * ROUND, r, :].bitcast(I32),
                        in_=stage[PACK * ROUND * r : PACK * ROUND * (r + 1), quadrant, :].bitcast(I32),
                    )

        def after_large(i):
            if i < 2 * (1 + ROUNDS):
                move_scales(i)

        def contract(first_pass, a, words):
            for j in range(words.shape[1]):
                g = first_pass + j
                r, plane = divmod(g, ROUND)
                for b in range(HALF_BANKS):
                    cols = slice(b * BANK_RANKS, (b + 1) * BANK_RANKS)
                    nc.tensor.matmul_mx(
                        out=acc[a][b][:],
                        lhsT=x_codes[:, g, :].bitcast(FP8X4),
                        lhsT_scale=x_planes[:, g, :],
                        rhs=words[:, j, cols].bitcast(FP8X4),
                        rhs_scale=in_planes[PACK * plane : P, r, a * HALF + cols.start : a * HALF + cols.stop],
                        start=(g == 0),
                        stop=(g == PASSES - 1),
                    )

        def load_half(first_pass, passes, a):
            w_half = half_pool.tile([P, LATE_LOAD, HALF], U32, align_bytes=64)
            nc.sync.dma_start(
                out=w_half[:, :passes, :].bitcast(I32),
                in_=in_words[first_pass : first_pass + passes, :, a * HALF : (a + 1) * HALF].rearrange(
                    "g p n -> p g n"
                ),
            )
            return w_half[:, :passes, :]

        y3_codes = keep.tile([P, HALVES, POS], U32, align_bytes=64)
        y3_planes = keep.tile([P, HALVES, POS], U8, align_bytes=64)

        def filter_and_quantise(a):
            y0 = work.tile([P, PACK, P], F32)
            for two_t in (slice(0, 2), slice(2, PACK)):
                for copy, b in ((nc.vector.tensor_copy, 0), (nc.scalar.copy, 1)):
                    copy(
                        out=y0[:, two_t, b * BANK_WORDS : (b + 1) * BANK_WORDS],
                        in_=acc[a][b][:].rearrange("q (p t) -> q t p", t=PACK)[:, two_t, :],
                    )
            before = []
            for t in range(PACK):
                turned = psum.tile([P, POS], F32, name="turned%d" % t, tag="bank")
                nc.tensor.transpose(turned[:], y0[:, t, :], reorder[:])
                before.append(turned[:])
            for stage_no, (f, run, step) in enumerate(AXES):
                after = work.tile([P, PACK, POS], F32, name="after%d" % f, tag="after%d" % f)
                tap, src, dst = [], [], []
                for t in range(PACK):
                    tap.append([
                        taps_sb[:, t, (f * TAPS + k) * HALVES + a : (f * TAPS + k) * HALVES + a + 1]
                        for k in range(TAPS)
                    ])
                    src.append(before[t].rearrange("p (o i) -> p o i", i=run))
                    dst.append(after[:, t, :].rearrange("p (o i) -> p o i", i=run))
                for pair in (range(0, 2), range(2, PACK)):
                    for t in pair:
                        nc.scalar.activation(out=dst[t], in_=src[t], func=COPY, scale=tap[t][1])
                    for t in pair:
                        nc.vector.scalar_tensor_tensor(
                            out=dst[t][:, :, step:], in0=src[t][:, :, : run - step], scalar=tap[t][0],
                            in1=dst[t][:, :, step:], op0=MULT, op1=ADD,
                        )
                    for t in pair:
                        nc.vector.scalar_tensor_tensor(
                            out=dst[t][:, :, : run - step], in0=src[t][:, :, step:], scalar=tap[t][2],
                            in1=dst[t][:, :, : run - step], op0=MULT, op1=ADD,
                        )
                before = [after[:, t, :] for t in range(PACK)]
                if a == HALVES - 1 and stage_no > 0:
                    warm = psum.tile([P, POS], F32, tag="bank")
                    for t in range(PACK if stage_no == 1 else 2):
                        nc.tensor.matmul(warm[:], lhsT=ident[:], rhs=before[t], start=True, stop=True)
            y3_grouped = work.tile([P, POS, PACK], BF16, align_bytes=64)
            nc.vector.tensor_copy(
                out=y3_grouped[:, : POS // 2, :], in_=after[:, :, : POS // 2].rearrange("p t n -> p n t")
            )
            nc.scalar.copy(out=y3_grouped[:, POS // 2 :, :], in_=after[:, :, POS // 2 :].rearrange("p t n -> p n t"))
            nc.vector.quantize_mx(
                out=y3_codes[:, a, :].bitcast(FP8X4),
                scales=y3_planes[:, a, :],
                in_=y3_grouped[:].rearrange("p n t -> p (n t)"),
            )

        def load_whole(first_pass):
            w_whole = whole_pool.tile([P, WHOLE_LOAD, RANK], U32, align_bytes=64)
            nc.sync.dma_start(
                out=w_whole[:].bitcast(I32),
                in_=in_words[first_pass : first_pass + WHOLE_LOAD].rearrange("g p n -> p g n"),
            )
            waiting.append((first_pass, w_whole))

        waiting = []
        for r in range(WHOLE_ROUNDS):
            for i, (load, arg) in enumerate(
                [(load_and_quantise_x, r)]
                + [(load_whole, first_pass) for first_pass in range(r * ROUND, (r + 1) * ROUND, WHOLE_LOAD)]
            ):
                load(arg)
                large = ROUND_LARGE * r + i
                after_large(large)
                ready = ((large + 1) // 2 - 1) * ROUND
                for first_pass, words in [item for item in waiting if item[0] < ready]:
                    for a in range(HALVES):
                        contract(first_pass, a, words[:, :, a * HALF : (a + 1) * HALF])
                waiting = [item for item in waiting if item[0] >= ready]
        for r in range(WHOLE_ROUNDS, ROUNDS):
            load_and_quantise_x(r)
            after_large(large + 1)
            large += 2
            for first_pass, passes in [(r * ROUND, 4)] if r < ROUNDS - 1 else [(PASSES - 4, 2), (PASSES - 2, 2)]:
                words = load_half(first_pass, passes, 0)
                after_large(large)
                contract(first_pass, 0, words)
        filter_and_quantise(0)
        for first_pass in range(WHOLE_ROUNDS * ROUND, PASSES - ROUND, LATE_LOAD):
            contract(first_pass, 1, load_half(first_pass, LATE_LOAD, 1))
        for first_pass, passes in ((PASSES - 4, 2), (PASSES - 2, 1), (PASSES - 1, 1)):
            contract(first_pass, 1, load_half(first_pass, passes, 1))
        uo_words = keep.tile([P, HALVES, COUT], U32, align_bytes=64)
        nc.sync.dma_start(out=uo_words[:].bitcast(I32), in_=out_words.rearrange("g p n -> p g n"))
        for quadrant in range(QUADRANTS):
            first = 32 * quadrant
            nc.sync.dma_start(
                out=out_planes[first : first + PACK * HALVES, :].bitcast(I32),
                in_=out_scales[:, PACK * quadrant : PACK * (quadrant + 1), :],
            )
        ctx.enter_context(
            tc.manual_schedule(
                engines={mybir.EngineType.DVE, mybir.EngineType.Activation, mybir.EngineType.PE}
            )
        )
        filter_and_quantise(1)

        out_ps = [psum.tile([P, POS], F32, name="out_ps%d" % m, tag="bank") for m in range(OUT_TILES)]
        for a in range(HALVES):
            for m in range(OUT_TILES):
                nc.tensor.matmul_mx(
                    out=out_ps[m][:],
                    lhsT=uo_words[:, a, m * P : (m + 1) * P].bitcast(FP8X4),
                    lhsT_scale=out_planes[PACK * a : P, m * P : (m + 1) * P],
                    rhs=y3_codes[:, a, :].bitcast(FP8X4),
                    rhs_scale=y3_planes[:, a, :],
                    start=(a == 0),
                    stop=(a == HALVES - 1),
                )
        out_sb = keep.tile([P, OUT_TILES, POS], F32)
        for m in range(OUT_TILES):
            src = out_ps[m][:].rearrange("i (o h) -> i h o", h=H)
            dst = out_sb[:, m, :].rearrange("i (h o) -> i h o", h=H)
            if m % 2 == 0:
                nc.vector.tensor_scalar_add(out=dst, in0=src, scalar1=bias_sb[:, m : m + 1])
            else:
                nc.scalar.activation(out=dst, in_=src, func=IDENTITY, bias=bias_sb[:, m : m + 1])
        for first in range(0, OUT_TILES, STORE_TILES):
            tiles = slice(first, first + STORE_TILES)
            nc.sync.dma_start(out=out_tiles[:, tiles, :], in_=out_sb[:, tiles, :])
